import numpy as np
import ml_dtypes


def mxq(x, axis, fmt="e4m3"):
    dtype, down = {"e4m3": (ml_dtypes.float8_e4m3fn, 7), "e5m2": (ml_dtypes.float8_e5m2, 14)}[fmt]
    v = np.moveaxis(np.asarray(x, np.float32).astype(ml_dtypes.bfloat16).astype(np.float64), axis, -1)
    blocks = v.reshape(v.shape[:-1] + (-1, 32))
    amax = np.abs(blocks).max(-1, keepdims=True)
    byte = np.maximum(np.where(amax > 0, np.frexp(amax)[1] - 1 + 127, 0) - down, 1)
    scale = np.exp2(byte - 127.0)
    codes = (blocks / scale).astype(np.float32).astype(dtype).astype(np.float64)
    return np.moveaxis((codes * scale).reshape(v.shape), -1, axis)


WIDE = False


def mx_kscale(k):
    if not WIDE:
        return np.ones(k)
    levels = np.array([10, -10, 5, -5, 0])
    if k % 512:
        return np.exp2(np.random.permutation(np.resize(levels, k // 32))).repeat(32)
    a = np.empty((k // 512, 16))
    for p in range(k // 512):
        a[p, :8] = np.random.permutation(np.resize(levels, 8))
        for g in range(8):
            far = levels[np.abs(levels - a[p, g]) >= 10]
            a[p, g + 8] = far[np.random.randint(len(far))]
    return np.exp2(a.ravel()).repeat(32)


BF16 = ml_dtypes.bfloat16


def bf(x):
    return np.asarray(x, np.float32).astype(BF16)


def f64(x):
    return np.asarray(x).astype(np.float64)


B, S, H, NH = 16, 256, 512, 16
LN_EPS = 1e-5


def silu(v):
    return v / (1.0 + np.exp(-v))


def setup_inputs():
    s, t = mx_kscale(H), mx_kscale(H)
    w = 1.0 / np.sqrt(H)
    z = (np.random.standard_normal((B, S, H)) + 0.3 * np.random.standard_normal((B, S, 1))) * 2.0 / S
    return {"z": bf(z),
            "hidden_states": bf(np.random.standard_normal((B, S, H)) * s),
            "Wg": bf(np.random.standard_normal((H, H)) * w / s[:, None]),
            "Wo": bf(np.random.standard_normal((H, H)) * w / t[:, None]),
            "gamma": bf((1.0 + 0.1 * np.random.standard_normal(H)) * t),
            "beta": bf(0.1 * np.random.standard_normal(H) * t)}


def reference(z, hidden_states, Wg, Wo, gamma, beta):
    z = f64(z)
    g = mxq(f64(hidden_states), 2, "e4m3") @ mxq(f64(Wg), 0, "e4m3")
    mu = np.mean(z, axis=-1, keepdims=True)
    var = np.mean(np.square(z - mu), axis=-1, keepdims=True)
    zn = (z - mu) * (1.0 / np.sqrt(var + LN_EPS)) * f64(gamma) + f64(beta)
    h = zn * silu(g)
    return mxq(h, 2, "e4m3") @ mxq(f64(Wo), 0, "e4m3")

@@ -1,0 +1,288 @@
+from contextlib import ExitStack
+
+import concourse.mybir as mybir
+from concourse.masks import make_identity
+
+F32 = mybir.dt.float32
+BF16 = mybir.dt.bfloat16
+U32 = mybir.dt.uint32
+U8 = mybir.dt.uint8
+FP8X4 = mybir.dt.float8_e4m3fn_x4
+ALU = mybir.AluOpType
+ACT = mybir.ActivationFunctionType
+
+P = 128
+PACK = 4
+H = 512
+TOKENS = 16 * 256
+TILES = 2
+CHUNK = TILES * P
+N_CHUNKS = TOKENS // CHUNK
+GROUPS = H // P
+HALVES = 2
+RUN = 4
+LN_EPS = 1e-5
+STORE_BUFS = 6
+
+FLOPS = 2 * 2 * TOKENS * H * H
+
+
+def tile_gatedlinearattention_pb_t_kernel(tc, z, hidden_states, Wg, Wo, gamma, beta, out):
+    nc = tc.nc
+
+    z_chunks = z.flatten_outer_dims().rearrange("(c p r) f -> c p (r f)", p=P, r=TILES)
+    hs_chunks = hidden_states.flatten_outer_dims().rearrange("(c p r) f -> c p (r f)", p=P, r=TILES)
+    out_chunks = out.flatten_outer_dims().rearrange("(c p r) f -> c p (r f)", p=P, r=TILES)
+
+    with ExitStack() as stack:
+        const = stack.enter_context(tc.tile_pool(name="const", bufs=1))
+        inputs = stack.enter_context(tc.tile_pool(name="inputs", bufs=N_CHUNKS))
+        work = stack.enter_context(tc.tile_pool(name="work", bufs=3))
+        stats = stack.enter_context(tc.tile_pool(name="stats", bufs=5))
+        stores = stack.enter_context(tc.tile_pool(name="stores", bufs=STORE_BUFS))
+        psum = stack.enter_context(tc.psum_pool(name="psum", bufs=2))
+
+        ident = const.tile([P, P], F32, name="ident")
+        make_identity(nc, ident[:])
+        minus_half = const.tile([P, TILES], F32, name="minus_half")
+        nc.gpsimd.memset(minus_half[:], -0.5)
+        table_warmer = const.tile([P, 1], F32, name="table_warmer")
+        nc.scalar.activation(out=table_warmer[:], in_=minus_half[:, 0:1], func=ACT.Silu)
+        gamma_raw = const.tile([P, GROUPS], BF16, name="gamma_raw")
+        beta_raw = const.tile([P, GROUPS], BF16, name="beta_raw")
+
+        z_sb = {}
+        hs_sb = {}
+
+        def load_chunk(c):
+            z_sb[c] = inputs.tile([P, TILES * H], BF16, name="z_sb")
+            nc.sync.dma_start(out=z_sb[c][:], in_=z_chunks[c])
+            hs_sb[c] = inputs.tile([P, TILES * H], BF16, name="hs_sb")
+            nc.sync.dma_start(out=hs_sb[c][:], in_=hs_chunks[c])
+
+        wg_raw = const.tile([P, PACK, H], BF16, name="wg_raw")
+        wo_raw = const.tile([P, PACK, H], BF16, name="wo_raw")
+
+        load_chunk(0)
+        nc.sync.dma_start(out=wg_raw[:], in_=Wg.rearrange("(p j) n -> p j n", j=PACK))
+        load_chunk(1)
+        nc.sync.dma_start(out=wo_raw[:], in_=Wo.rearrange("(p j) n -> p j n", j=PACK))
+        nc.sync.dma_start(out=gamma_raw[:], in_=gamma.rearrange("(p j) -> p j", j=GROUPS))
+        nc.sync.dma_start(out=beta_raw[:], in_=beta.rearrange("(p j) -> p j", j=GROUPS))
+        for c in range(2, N_CHUNKS):
+            load_chunk(c)
+
+        def regroup_wg():
+            grouped = const.tile([P, H, PACK], BF16, name="wg_grouped", align_bytes=64)
+            nc.vector.tensor_copy(
+                out=grouped[:].rearrange("p (j m) t -> p j m t", j=GROUPS),
+                in_=wg_raw[:].rearrange("p t (m j) -> p j m t", j=GROUPS),
+            )
+            return grouped
+
+        def regroup_wo():
+            grouped = const.tile([P, H, PACK], BF16, name="wo_grouped", align_bytes=64)
+            nc.scalar.copy(out=grouped[:], in_=wo_raw[:].rearrange("p t n -> p n t"))
+            return grouped
+
+        def quantise_weight(grouped, name):
+            codes = const.tile([P, H], U32, name=name + "_codes", align_bytes=64)
+            scales = const.tile([P, H], U8, name=name + "_scales", align_bytes=64)
+            nc.vector.quantize_mx(
+                out=codes[:].bitcast(FP8X4),
+                scales=scales[:],
+                in_=grouped[:].rearrange("p n t -> p (n t)"),
+            )
+            return codes, scales
+
+        def spread_gamma_beta():
+            gb = const.tile([P, 2 * GROUPS], F32, name="gb")
+            nc.gpsimd.tensor_copy(out=gb[:, 0:GROUPS], in_=gamma_raw[:])
+            nc.gpsimd.tensor_copy(out=gb[:, GROUPS : 2 * GROUPS], in_=beta_raw[:])
+            return gb
+
+        mean_var = {}
+        rstd = {}
+        zc = {}
+        zcT_ps = {}
+        hsT_ps = {}
+        hs_grouped = {}
+        hs_mx = {}
+        g_ps = {}
+        gate = {}
+        zn = {}
+        h_grouped = {}
+        h_mx = {}
+        out_ps = {}
+        weights = {}
+
+        def token_statistics(c):
+            partial = stats.tile([P, TILES, 6], F32, name="partial")
+            mean_var[c] = stats.tile([P, TILES, 2], F32, name="mean_var")
+            for r in range(TILES):
+                nc.vector.bn_stats(out=partial[:, r, :], in_=z_sb[c][:, r * H : (r + 1) * H])
+            for r in range(TILES):
+                nc.vector.bn_aggr(out=mean_var[c][:, r, :], in_=partial[:, r, :])
+            var_eps = stats.tile([P, TILES], F32, name="var_eps")
+            nc.gpsimd.tensor_scalar(
+                out=var_eps[:], in0=mean_var[c][:, :, 1], scalar1=LN_EPS, scalar2=None, op0=ALU.add
+            )
+            rstd[c] = stats.tile([P, TILES], F32, name="rstd")
+            nc.gpsimd.tensor_tensor(out=rstd[c][:], in0=var_eps[:], in1=minus_half[:], op=ALU.pow)
+
+        def centre_and_scale(c, r):
+            if r == 0:
+                zc[c] = work.tile([P, TILES, H], F32, name="zc")
+            nc.vector.tensor_scalar(
+                out=zc[c][:, r, :].rearrange("p (j m) -> p j m", j=GROUPS),
+                in0=z_sb[c][:, r * H : (r + 1) * H].rearrange("p (m j) -> p j m", j=GROUPS),
+                scalar1=mean_var[c][:, r, 0:1],
+                scalar2=rstd[c][:, r : r + 1],
+                op0=ALU.subtract,
+                op1=ALU.mult,
+            )
+
+        def transpose_zc(c):
+            for pair in range(GROUPS // 2):
+                zcT_ps[c, pair] = psum.tile([P, 2, CHUNK], F32, name="zcT_ps")
+                for i in range(2):
+                    j = 2 * pair + i
+                    for r in range(TILES):
+                        nc.tensor.transpose(
+                            zcT_ps[c, pair][:, i, r * P : (r + 1) * P],
+                            zc[c][:, r, j * P : (j + 1) * P],
+                            ident[:],
+                        )
+
+        def transpose_hs(c):
+            words = hs_sb[c][:].bitcast(F32)
+            hsT_ps[c] = psum.tile([P, HALVES, CHUNK], F32, name="hsT_ps")
+            for r in range(TILES):
+                for u in range(HALVES):
+                    nc.tensor.transpose(
+                        hsT_ps[c][:, u, r * P : (r + 1) * P],
+                        words[:, r * H // HALVES + u : (r + 1) * H // HALVES : HALVES],
+                        ident[:],
+                    )
+
+        def regroup_hs(c):
+            hs_grouped[c] = work.tile([P, CHUNK * PACK], BF16, name="hs_grouped", align_bytes=64)
+            copy = nc.vector.tensor_copy if c % 2 == 0 else nc.scalar.copy
+            copy(
+                out=hs_grouped[c][:].bitcast(F32).rearrange("p (w u) -> p w u", u=HALVES),
+                in_=hsT_ps[c][:].rearrange("p u w -> p w u"),
+            )
+
+        def quantise(grouped, name):
+            codes = work.tile([P, CHUNK], U32, name=name + "_codes", align_bytes=64)
+            scales = work.tile([P, CHUNK], U8, name=name + "_scales", align_bytes=64)
+            nc.vector.quantize_mx(out=codes[:].bitcast(FP8X4), scales=scales[:], in_=grouped[:])
+            return codes, scales
+
+        def first_product(c):
+            wg_codes, wg_scales = weights["wg"]
+            hs_codes, hs_scales = hs_mx[c]
+            for pair in range(GROUPS // 2):
+                g_ps[c, pair] = psum.tile([P, 2, CHUNK], F32, name="g_ps")
+                for i in range(2):
+                    j = 2 * pair + i
+                    nc.tensor.matmul_mx(
+                        out=g_ps[c, pair][:, i, :],
+                        lhsT=wg_codes[:, j * P : (j + 1) * P].bitcast(FP8X4),
+                        lhsT_scale=wg_scales[:, j * P : (j + 1) * P],
+                        rhs=hs_codes[:].bitcast(FP8X4),
+                        rhs_scale=hs_scales[:],
+                        start=True,
+                        stop=True,
+                    )
+
+        def silu_gate(c):
+            gate[c] = work.tile([P, GROUPS, CHUNK], F32, name="gate")
+            for pair in range(GROUPS // 2):
+                nc.scalar.activation(
+                    out=gate[c][:, 2 * pair : 2 * pair + 2, :], in_=g_ps[c, pair][:], func=ACT.Silu
+                )
+
+        def gamma_beta(c):
+            gb = weights["gb"]
+            zn[c] = work.tile([P, GROUPS, CHUNK], F32, name="zn")
+            for j in range(GROUPS):
+                nc.scalar.activation(
+                    out=zn[c][:, j, :],
+                    in_=zcT_ps[c, j // 2][:, j % 2, :],
+                    func=ACT.Identity,
+                    scale=gb[:, j : j + 1],
+                    bias=gb[:, GROUPS + j : GROUPS + j + 1],
+                )
+
+        def gated(c):
+            h_grouped[c] = work.tile([P, CHUNK * PACK], BF16, name="h_grouped", align_bytes=64)
+            nc.vector.tensor_tensor(
+                out=h_grouped[c][:].rearrange("p (a i j) -> p a j i", i=RUN, j=PACK),
+                in0=zn[c][:].rearrange("p j (a i) -> p a j i", i=RUN),
+                in1=gate[c][:].rearrange("p j (a i) -> p a j i", i=RUN),
+                op=ALU.mult,
+            )
+
+        def second_product(c):
+            wo_codes, wo_scales = weights["wo"]
+            h_codes, h_scales = h_mx[c]
+            for r in range(TILES):
+                out_ps[c, r] = psum.tile([P, H], F32, name="out_ps")
+                nc.tensor.matmul_mx(
+                    out=out_ps[c, r][:],
+                    lhsT=h_codes[:, r * P : (r + 1) * P].bitcast(FP8X4),
+                    lhsT_scale=h_scales[:, r * P : (r + 1) * P],
+                    rhs=wo_codes[:].bitcast(FP8X4),
+                    rhs_scale=wo_scales[:],
+                    start=True,
+                    stop=True,
+                )
+
+        def store(c):
+            out_sb = stores.tile([P, TILES * H], F32, name="out_sb")
+            for r in range(TILES):
+                nc.scalar.copy(out=out_sb[:, r * H : (r + 1) * H], in_=out_ps[c, r][:])
+            nc.sync.dma_start(out=out_chunks[c], in_=out_sb[:])
+
+        def live(c):
+            return 0 <= c < N_CHUNKS
+
+        def step(t):
+            if live(t + 2):
+                regroup_hs(t + 2)
+                centre_and_scale(t + 2, 0)
+            if live(t):
+                h_mx[t] = quantise(h_grouped[t], "h")
+            if live(t + 2):
+                centre_and_scale(t + 2, 1)
+                hs_mx[t + 2] = quantise(hs_grouped[t + 2], "hs")
+            if live(t + 1):
+                silu_gate(t + 1)
+            if live(t):
+                second_product(t)
+            if live(t + 2):
+                first_product(t + 2)
+            if live(t + 1):
+                gamma_beta(t + 1)
+            if live(t + 2):
+                transpose_zc(t + 2)
+            if live(t + 3):
+                transpose_hs(t + 3)
+            if live(t + 4):
+                token_statistics(t + 4)
+            if live(t):
+                store(t)
+            if live(t + 1):
+                gated(t + 1)
+
+        step(-4)
+        wg_grouped = regroup_wg()
+        step(-3)
+        weights["wg"] = quantise_weight(wg_grouped, "wg")
+        wo_grouped = regroup_wo()
+        weights["gb"] = spread_gamma_beta()
+        step(-2)
+        weights["wo"] = quantise_weight(wo_grouped, "wo")
+        for t in range(-1, N_CHUNKS):
+            step(t)

@@ -197,19 +197,21 @@ def tile_gatedlinearattention_pb_t_kernel(tc, z, hidden_states, Wg, Wo, gamma, b
                     )
 
         def silu_gate(c):
-            gate[c] = work.tile([P, GROUPS, CHUNK], F32, name="gate")
+            gate[c] = work.tile([P, CHUNK // RUN, GROUPS, RUN], F32, name="gate")
             for pair in range(GROUPS // 2):
                 nc.scalar.activation(
-                    out=gate[c][:, 2 * pair : 2 * pair + 2, :], in_=g_ps[c, pair][:], func=ACT.Silu
+                    out=gate[c][:, :, 2 * pair : 2 * pair + 2, :].rearrange("p a j i -> p j a i"),
+                    in_=g_ps[c, pair][:].rearrange("p j (a i) -> p j a i", i=RUN),
+                    func=ACT.Silu,
                 )
 
         def gamma_beta(c):
             gb = weights["gb"]
-            zn[c] = work.tile([P, GROUPS, CHUNK], F32, name="zn")
+            zn[c] = work.tile([P, CHUNK // RUN, GROUPS, RUN], F32, name="zn")
             for j in range(GROUPS):
                 nc.scalar.activation(
-                    out=zn[c][:, j, :],
-                    in_=zcT_ps[c, j // 2][:, j % 2, :],
+                    out=zn[c][:, :, j, :],
+                    in_=zcT_ps[c, j // 2][:, j % 2, :].rearrange("p (a i) -> p a i", i=RUN),
                     func=ACT.Identity,
                     scale=gb[:, j : j + 1],
                     bias=gb[:, GROUPS + j : GROUPS + j + 1],
@@ -219,8 +221,8 @@ def tile_gatedlinearattention_pb_t_kernel(tc, z, hidden_states, Wg, Wo, gamma, b
             h_grouped[c] = work.tile([P, CHUNK * PACK], BF16, name="h_grouped", align_bytes=64)
             nc.vector.tensor_tensor(
                 out=h_grouped[c][:].rearrange("p (a i j) -> p a j i", i=RUN, j=PACK),
-                in0=zn[c][:].rearrange("p j (a i) -> p a j i", i=RUN),
-                in1=gate[c][:].rearrange("p j (a i) -> p a j i", i=RUN),
+                in0=zn[c][:],
+                in1=gate[c][:],
                 op=ALU.mult,
             )
 

@@ -15,6 +15,7 @@ P = 128
 PACK = 4
 H = 512
 TOKENS = 16 * 256
+HALF = H // 2
 TILES = 2
 CHUNK = TILES * P
 N_CHUNKS = TOKENS // CHUNK
@@ -38,7 +39,7 @@ def tile_gatedlinearattention_pb_t_kernel(tc, z, hidden_states, Wg, Wo, gamma, b
         const = stack.enter_context(tc.tile_pool(name="const", bufs=1))
         inputs = stack.enter_context(tc.tile_pool(name="inputs", bufs=N_CHUNKS))
         work = stack.enter_context(tc.tile_pool(name="work", bufs=3))
-        stats = stack.enter_context(tc.tile_pool(name="stats", bufs=5))
+        stats = stack.enter_context(tc.tile_pool(name="stats", bufs=6))
         stores = stack.enter_context(tc.tile_pool(name="stores", bufs=STORE_BUFS))
         psum = stack.enter_context(tc.psum_pool(name="psum", bufs=2))
 
@@ -46,61 +47,70 @@ def tile_gatedlinearattention_pb_t_kernel(tc, z, hidden_states, Wg, Wo, gamma, b
         make_identity(nc, ident[:])
         minus_half = const.tile([P, TILES], F32, name="minus_half")
         nc.gpsimd.memset(minus_half[:], -0.5)
-        table_warmer = const.tile([P, 1], F32, name="table_warmer")
-        nc.scalar.activation(out=table_warmer[:], in_=minus_half[:, 0:1], func=ACT.Silu)
         gamma_raw = const.tile([P, GROUPS], BF16, name="gamma_raw")
         beta_raw = const.tile([P, GROUPS], BF16, name="beta_raw")
+        gamma_col = const.tile([P, GROUPS], F32, name="gamma_col")
+        beta_col = const.tile([P, GROUPS], F32, name="beta_col")
 
         z_sb = {}
         hs_sb = {}
 
-        def load_chunk(c):
+        def load_z(c):
             z_sb[c] = inputs.tile([P, TILES * H], BF16, name="z_sb")
             nc.sync.dma_start(out=z_sb[c][:], in_=z_chunks[c])
+
+        def load_hs(c):
             hs_sb[c] = inputs.tile([P, TILES * H], BF16, name="hs_sb")
             nc.sync.dma_start(out=hs_sb[c][:], in_=hs_chunks[c])
 
         wg_raw = const.tile([P, PACK, H], BF16, name="wg_raw")
         wo_raw = const.tile([P, PACK, H], BF16, name="wo_raw")
-
-        load_chunk(0)
+        load_z(0)
+        nc.scalar.dma_start(out=gamma_raw[:], in_=gamma.rearrange("(p j) -> p j", j=GROUPS))
+        nc.scalar.dma_start(out=beta_raw[:], in_=beta.rearrange("(p j) -> p j", j=GROUPS))
+        load_hs(0)
         nc.sync.dma_start(out=wg_raw[:], in_=Wg.rearrange("(p j) n -> p j n", j=PACK))
-        load_chunk(1)
+        load_z(1)
+        load_hs(1)
         nc.sync.dma_start(out=wo_raw[:], in_=Wo.rearrange("(p j) n -> p j n", j=PACK))
-        nc.sync.dma_start(out=gamma_raw[:], in_=gamma.rearrange("(p j) -> p j", j=GROUPS))
-        nc.sync.dma_start(out=beta_raw[:], in_=beta.rearrange("(p j) -> p j", j=GROUPS))
         for c in range(2, N_CHUNKS):
-            load_chunk(c)
+            load_z(c)
+            load_hs(c)
 
-        def regroup_wg():
-            grouped = const.tile([P, H, PACK], BF16, name="wg_grouped", align_bytes=64)
-            nc.vector.tensor_copy(
-                out=grouped[:].rearrange("p (j m) t -> p j m t", j=GROUPS),
-                in_=wg_raw[:].rearrange("p t (m j) -> p j m t", j=GROUPS),
+        table_warmer = const.tile([P, 1], F32, name="table_warmer")
+        nc.scalar.activation(out=table_warmer[:], in_=minus_half[:, 0:1], func=ACT.Silu)
+        nc.gpsimd.tensor_copy(out=gamma_col[:], in_=gamma_raw[:])
+        nc.gpsimd.tensor_copy(out=beta_col[:], in_=beta_raw[:])
+
+        wg_grouped = const.tile([P, H, PACK], BF16, name="wg_grouped", align_bytes=64)
+        wg_codes = const.tile([P, H], U32, name="wg_codes", align_bytes=64)
+        wg_scales = const.tile([P, H], U8, name="wg_scales", align_bytes=64)
+        wo_grouped = const.tile([P, H, PACK], BF16, name="wo_grouped", align_bytes=64)
+        wo_codes = const.tile([P, H], U32, name="wo_codes", align_bytes=64)
+        wo_scales = const.tile([P, H], U8, name="wo_scales", align_bytes=64)
+
+        def regroup_wg(copy, half):
+            copy(
+                out=wg_grouped[:, half * HALF : (half + 1) * HALF, :].rearrange("p (j m) t -> p j m t", j=2),
+                in_=wg_raw[:].rearrange("p t (m j) -> p j m t", j=GROUPS)[:, 2 * half : 2 * half + 2],
             )
-            return grouped
 
-        def regroup_wo():
-            grouped = const.tile([P, H, PACK], BF16, name="wo_grouped", align_bytes=64)
-            nc.scalar.copy(out=grouped[:], in_=wo_raw[:].rearrange("p t n -> p n t"))
-            return grouped
+        def regroup_wo(copy, half):
+            cols = slice(half * HALF, (half + 1) * HALF)
+            copy(
+                out=wo_grouped[:, cols, :].rearrange("p (a i) t -> p a t i", i=RUN),
+                in_=wo_raw[:, :, cols].rearrange("p t (a i) -> p a t i", i=RUN),
+            )
 
-        def quantise_weight(grouped, name):
-            codes = const.tile([P, H], U32, name=name + "_codes", align_bytes=64)
-            scales = const.tile([P, H], U8, name=name + "_scales", align_bytes=64)
+        def quantise_weight(grouped, codes, scales, half):
+            cols = slice(half * HALF, (half + 1) * HALF)
             nc.vector.quantize_mx(
-                out=codes[:].bitcast(FP8X4),
-                scales=scales[:],
-                in_=grouped[:].rearrange("p n t -> p (n t)"),
+                out=codes[:, cols].bitcast(FP8X4),
+                scales=scales[:, cols],
+                in_=grouped[:, cols, :].rearrange("p n t -> p (n t)"),
             )
-            return codes, scales
 
-        def spread_gamma_beta():
-            gb = const.tile([P, 2 * GROUPS], F32, name="gb")
-            nc.gpsimd.tensor_copy(out=gb[:, 0:GROUPS], in_=gamma_raw[:])
-            nc.gpsimd.tensor_copy(out=gb[:, GROUPS : 2 * GROUPS], in_=beta_raw[:])
-            return gb
-
+        partial = {}
         mean_var = {}
         rstd = {}
         zc = {}
@@ -114,15 +124,17 @@ def tile_gatedlinearattention_pb_t_kernel(tc, z, hidden_states, Wg, Wo, gamma, b
         h_grouped = {}
         h_mx = {}
         out_ps = {}
-        weights = {}
+        out_sb = {}
+
+        def token_sums(c, r):
+            if r == 0:
+                partial[c] = stats.tile([P, TILES, 6], F32, name="partial")
+            nc.vector.bn_stats(out=partial[c][:, r, :], in_=z_sb[c][:, r * H : (r + 1) * H])
 
         def token_statistics(c):
-            partial = stats.tile([P, TILES, 6], F32, name="partial")
             mean_var[c] = stats.tile([P, TILES, 2], F32, name="mean_var")
             for r in range(TILES):
-                nc.vector.bn_stats(out=partial[:, r, :], in_=z_sb[c][:, r * H : (r + 1) * H])
-            for r in range(TILES):
-                nc.vector.bn_aggr(out=mean_var[c][:, r, :], in_=partial[:, r, :])
+                nc.vector.bn_aggr(out=mean_var[c][:, r, :], in_=partial[c][:, r, :])
             var_eps = stats.tile([P, TILES], F32, name="var_eps")
             nc.gpsimd.tensor_scalar(
                 out=var_eps[:], in0=mean_var[c][:, :, 1], scalar1=LN_EPS, scalar2=None, op0=ALU.add
@@ -142,17 +154,16 @@ def tile_gatedlinearattention_pb_t_kernel(tc, z, hidden_states, Wg, Wo, gamma, b
                 op1=ALU.mult,
             )
 
-        def transpose_zc(c):
-            for pair in range(GROUPS // 2):
-                zcT_ps[c, pair] = psum.tile([P, 2, CHUNK], F32, name="zcT_ps")
-                for i in range(2):
-                    j = 2 * pair + i
-                    for r in range(TILES):
-                        nc.tensor.transpose(
-                            zcT_ps[c, pair][:, i, r * P : (r + 1) * P],
-                            zc[c][:, r, j * P : (j + 1) * P],
-                            ident[:],
-                        )
+        def transpose_zc(c, pair):
+            zcT_ps[c, pair] = psum.tile([P, 2, CHUNK], F32, name="zcT_ps")
+            for i in range(2):
+                j = 2 * pair + i
+                for r in range(TILES):
+                    nc.tensor.transpose(
+                        zcT_ps[c, pair][:, i, r * P : (r + 1) * P],
+                        zc[c][:, r, j * P : (j + 1) * P],
+                        ident[:],
+                    )
 
         def transpose_hs(c):
             words = hs_sb[c][:].bitcast(F32)
@@ -165,9 +176,8 @@ def tile_gatedlinearattention_pb_t_kernel(tc, z, hidden_states, Wg, Wo, gamma, b
                         ident[:],
                     )
 
-        def regroup_hs(c):
+        def regroup_hs(c, copy):
             hs_grouped[c] = work.tile([P, CHUNK * PACK], BF16, name="hs_grouped", align_bytes=64)
-            copy = nc.vector.tensor_copy if c % 2 == 0 else nc.scalar.copy
             copy(
                 out=hs_grouped[c][:].bitcast(F32).rearrange("p (w u) -> p w u", u=HALVES),
                 in_=hsT_ps[c][:].rearrange("p u w -> p w u"),
@@ -179,112 +189,184 @@ def tile_gatedlinearattention_pb_t_kernel(tc, z, hidden_states, Wg, Wo, gamma, b
             nc.vector.quantize_mx(out=codes[:].bitcast(FP8X4), scales=scales[:], in_=grouped[:])
             return codes, scales
 
-        def first_product(c):
-            wg_codes, wg_scales = weights["wg"]
+        def quantise_h(c):
+            codes = work.tile([P, CHUNK], U32, name="h_codes", align_bytes=64)
+            scales = work.tile([P, CHUNK], U8, name="h_scales", align_bytes=64)
+            for first, tokens in pieces(c):
+                cols = slice(first, first + tokens)
+                nc.vector.quantize_mx(
+                    out=codes[:, cols].bitcast(FP8X4),
+                    scales=scales[:, cols],
+                    in_=h_grouped[c][:, first * PACK : (first + tokens) * PACK],
+                )
+            h_mx[c] = codes, scales
+
+        def first_product(c, pair):
             hs_codes, hs_scales = hs_mx[c]
-            for pair in range(GROUPS // 2):
-                g_ps[c, pair] = psum.tile([P, 2, CHUNK], F32, name="g_ps")
-                for i in range(2):
-                    j = 2 * pair + i
-                    nc.tensor.matmul_mx(
-                        out=g_ps[c, pair][:, i, :],
-                        lhsT=wg_codes[:, j * P : (j + 1) * P].bitcast(FP8X4),
-                        lhsT_scale=wg_scales[:, j * P : (j + 1) * P],
-                        rhs=hs_codes[:].bitcast(FP8X4),
-                        rhs_scale=hs_scales[:],
-                        start=True,
-                        stop=True,
-                    )
-
-        def silu_gate(c):
-            gate[c] = work.tile([P, CHUNK // RUN, GROUPS, RUN], F32, name="gate")
-            for pair in range(GROUPS // 2):
-                nc.scalar.activation(
-                    out=gate[c][:, :, 2 * pair : 2 * pair + 2, :].rearrange("p a j i -> p j a i"),
-                    in_=g_ps[c, pair][:].rearrange("p j (a i) -> p j a i", i=RUN),
-                    func=ACT.Silu,
-                )
-
-        def gamma_beta(c):
-            gb = weights["gb"]
-            zn[c] = work.tile([P, CHUNK // RUN, GROUPS, RUN], F32, name="zn")
-            for j in range(GROUPS):
-                nc.scalar.activation(
-                    out=zn[c][:, :, j, :],
-                    in_=zcT_ps[c, j // 2][:, j % 2, :].rearrange("p (a i) -> p a i", i=RUN),
-                    func=ACT.Identity,
-                    scale=gb[:, j : j + 1],
-                    bias=gb[:, GROUPS + j : GROUPS + j + 1],
-                )
-
-        def gated(c):
-            h_grouped[c] = work.tile([P, CHUNK * PACK], BF16, name="h_grouped", align_bytes=64)
-            nc.vector.tensor_tensor(
-                out=h_grouped[c][:].rearrange("p (a i j) -> p a j i", i=RUN, j=PACK),
-                in0=zn[c][:],
-                in1=gate[c][:],
-                op=ALU.mult,
-            )
-
-        def second_product(c):
-            wo_codes, wo_scales = weights["wo"]
-            h_codes, h_scales = h_mx[c]
-            for r in range(TILES):
-                out_ps[c, r] = psum.tile([P, H], F32, name="out_ps")
+            g_ps[c, pair] = psum.tile([P, 2, CHUNK], F32, name="g_ps")
+            for i in range(2):
+                j = 2 * pair + i
                 nc.tensor.matmul_mx(
-                    out=out_ps[c, r][:],
-                    lhsT=h_codes[:, r * P : (r + 1) * P].bitcast(FP8X4),
-                    lhsT_scale=h_scales[:, r * P : (r + 1) * P],
-                    rhs=wo_codes[:].bitcast(FP8X4),
-                    rhs_scale=wo_scales[:],
+                    out=g_ps[c, pair][:, i, :],
+                    lhsT=wg_codes[:, j * P : (j + 1) * P].bitcast(FP8X4),
+                    lhsT_scale=wg_scales[:, j * P : (j + 1) * P],
+                    rhs=hs_codes[:].bitcast(FP8X4),
+                    rhs_scale=hs_scales[:],
                     start=True,
                     stop=True,
                 )
 
+        def silu_gate(c, pair):
+            if pair == 0:
+                gate[c] = work.tile([P, CHUNK // RUN, GROUPS, RUN], F32, name="gate")
+            nc.scalar.activation(
+                out=gate[c][:, :, 2 * pair : 2 * pair + 2, :].rearrange("p a j i -> p j a i"),
+                in_=g_ps[c, pair][:].rearrange("p j (a i) -> p j a i", i=RUN),
+                func=ACT.Silu,
+            )
+
+        def gamma_beta(c, pair):
+            if pair == 0:
+                zn[c] = work.tile([P, CHUNK // RUN, GROUPS, RUN], F32, name="zn")
+            for i in range(2):
+                j = 2 * pair + i
+                nc.scalar.activation(
+                    out=zn[c][:, :, j, :],
+                    in_=zcT_ps[c, pair][:, i, :].rearrange("p (a i) -> p a i", i=RUN),
+                    func=ACT.Identity,
+                    scale=gamma_col[:, j : j + 1],
+                    bias=beta_col[:, j : j + 1],
+                )
+
+        def pieces(c):
+            return [(0, CHUNK)] if c < N_CHUNKS - 1 else [(r * P, P) for r in range(TILES)]
+
+        def gated(c):
+            h_grouped[c] = work.tile([P, CHUNK * PACK], BF16, name="h_grouped", align_bytes=64)
+            for first, tokens in pieces(c):
+                runs = slice(first // RUN, (first + tokens) // RUN)
+                nc.vector.tensor_tensor(
+                    out=h_grouped[c][:, first * PACK : (first + tokens) * PACK].rearrange(
+                        "p (a i j) -> p a j i", i=RUN, j=PACK
+                    ),
+                    in0=zn[c][:, runs],
+                    in1=gate[c][:, runs],
+                    op=ALU.mult,
+                )
+
+        def second_product(c, r):
+            h_codes, h_scales = h_mx[c]
+            out_ps[c, r] = psum.tile([P, H], F32, name="out_ps")
+            nc.tensor.matmul_mx(
+                out=out_ps[c, r][:],
+                lhsT=h_codes[:, r * P : (r + 1) * P].bitcast(FP8X4),
+                lhsT_scale=h_scales[:, r * P : (r + 1) * P],
+                rhs=wo_codes[:].bitcast(FP8X4),
+                rhs_scale=wo_scales[:],
+                start=True,
+                stop=True,
+            )
+
+        def empty_out(c, r, copy):
+            if r == 0:
+                out_sb[c] = stores.tile([P, TILES * H], F32, name="out_sb")
+            copy(out=out_sb[c][:, r * H : (r + 1) * H], in_=out_ps[c, r][:])
+
         def store(c):
-            out_sb = stores.tile([P, TILES * H], F32, name="out_sb")
-            for r in range(TILES):
-                nc.scalar.copy(out=out_sb[:, r * H : (r + 1) * H], in_=out_ps[c, r][:])
-            nc.sync.dma_start(out=out_chunks[c], in_=out_sb[:])
+            if c < N_CHUNKS - 1:
+                nc.sync.dma_start(out=out_chunks[c], in_=out_sb[c][:])
+            else:
+                nc.scalar.dma_start(out=out_chunks[c][:, 0:H], in_=out_sb[c][:, 0:H])
+                nc.sync.dma_start(out=out_chunks[c][:, H : 2 * H], in_=out_sb[c][:, H : 2 * H])
+
+        vcopy = nc.vector.tensor_copy
+        scopy = nc.scalar.copy
 
         def live(c):
             return 0 <= c < N_CHUNKS
 
+        def hs_copy(c):
+            return scopy if c < 4 or c % 2 else vcopy
+
         def step(t):
             if live(t + 2):
-                regroup_hs(t + 2)
+                regroup_hs(t + 2, hs_copy(t + 2))
                 centre_and_scale(t + 2, 0)
-            if live(t):
-                h_mx[t] = quantise(h_grouped[t], "h")
+            quantise_h(t)
             if live(t + 2):
                 centre_and_scale(t + 2, 1)
                 hs_mx[t + 2] = quantise(hs_grouped[t + 2], "hs")
             if live(t + 1):
-                silu_gate(t + 1)
-            if live(t):
-                second_product(t)
+                silu_gate(t + 1, 0)
+                silu_gate(t + 1, 1)
+            second_product(t, 0)
+            second_product(t, 1)
             if live(t + 2):
-                first_product(t + 2)
+                first_product(t + 2, 0)
+                first_product(t + 2, 1)
             if live(t + 1):
-                gamma_beta(t + 1)
+                gamma_beta(t + 1, 0)
+                gamma_beta(t + 1, 1)
             if live(t + 2):
-                transpose_zc(t + 2)
+                transpose_zc(t + 2, 0)
+                transpose_zc(t + 2, 1)
             if live(t + 3):
                 transpose_hs(t + 3)
             if live(t + 4):
+                token_sums(t + 4, 0)
+                token_sums(t + 4, 1)
                 token_statistics(t + 4)
-            if live(t):
-                store(t)
+            empty_out(t, 0, scopy)
+            empty_out(t, 1, scopy if t < N_CHUNKS - 4 else vcopy)
+            store(t)
             if live(t + 1):
                 gated(t + 1)
 
-        step(-4)
-        wg_grouped = regroup_wg()
-        step(-3)
-        weights["wg"] = quantise_weight(wg_grouped, "wg")
-        wo_grouped = regroup_wo()
-        weights["gb"] = spread_gamma_beta()
-        step(-2)
-        weights["wo"] = quantise_weight(wo_grouped, "wo")
-        for t in range(-1, N_CHUNKS):
+        with tc.manual_schedule():
+            token_sums(0, 0)
+            token_sums(0, 1)
+            token_statistics(0)
+            transpose_hs(0)
+            regroup_wg(vcopy, 0)
+            regroup_wg(scopy, 1)
+            quantise_weight(wg_grouped, wg_codes, wg_scales, 0)
+            quantise_weight(wg_grouped, wg_codes, wg_scales, 1)
+            regroup_hs(0, hs_copy(0))
+            hs_mx[0] = quantise(hs_grouped[0], "hs")
+            transpose_hs(1)
+            token_sums(1, 0)
+            token_sums(1, 1)
+            token_statistics(1)
+            centre_and_scale(0, 0)
+            centre_and_scale(0, 1)
+            first_product(0, 0)
+            first_product(0, 1)
+            regroup_hs(1, hs_copy(1))
+            transpose_zc(0, 0)
+            transpose_zc(0, 1)
+            silu_gate(0, 0)
+            silu_gate(0, 1)
+            hs_mx[1] = quantise(hs_grouped[1], "hs")
+            token_sums(2, 0)
+            token_sums(2, 1)
+            token_statistics(2)
+            gamma_beta(0, 0)
+            gamma_beta(0, 1)
+            centre_and_scale(1, 0)
+            centre_and_scale(1, 1)
+            regroup_wo(scopy, 0)
+            first_product(1, 0)
+            first_product(1, 1)
+            transpose_zc(1, 0)
+            transpose_zc(1, 1)
+            transpose_hs(2)
+            token_sums(3, 0)
+            token_sums(3, 1)
+            token_statistics(3)
+            regroup_wo(scopy, 1)
+            gated(0)
+            quantise_weight(wo_grouped, wo_codes, wo_scales, 0)
+            quantise_weight(wo_grouped, wo_codes, wo_scales, 1)
+
+        for t in range(N_CHUNKS):
             step(t)

@@ -23,6 +23,7 @@ GROUPS = H // P
 HALVES = 2
 RUN = 4
 LN_EPS = 1e-5
+GROUP_STARTS = [0, 1] + list(range(2, N_CHUNKS + 1, 2))
 STORE_BUFS = 6
 
 FLOPS = 2 * 2 * TOKENS * H * H
@@ -45,7 +46,7 @@ def tile_gatedlinearattention_pb_t_kernel(tc, z, hidden_states, Wg, Wo, gamma, b
 
         ident = const.tile([P, P], F32, name="ident")
         make_identity(nc, ident[:])
-        minus_half = const.tile([P, TILES], F32, name="minus_half")
+        minus_half = const.tile([P, 2 * TILES], F32, name="minus_half")
         nc.gpsimd.memset(minus_half[:], -0.5)
         gamma_raw = const.tile([P, GROUPS], BF16, name="gamma_raw")
         beta_raw = const.tile([P, GROUPS], BF16, name="beta_raw")
@@ -113,6 +114,7 @@ def tile_gatedlinearattention_pb_t_kernel(tc, z, hidden_states, Wg, Wo, gamma, b
         partial = {}
         mean_var = {}
         rstd = {}
+        group_of = {}
         zc = {}
         zcT_ps = {}
         hsT_ps = {}
@@ -132,24 +134,36 @@ def tile_gatedlinearattention_pb_t_kernel(tc, z, hidden_states, Wg, Wo, gamma, b
             nc.vector.bn_stats(out=partial[c][:, r, :], in_=z_sb[c][:, r * H : (r + 1) * H])
 
         def token_statistics(c):
-            mean_var[c] = stats.tile([P, TILES, 2], F32, name="mean_var")
+            if c in GROUP_STARTS:
+                size = TILES * (GROUP_STARTS[GROUP_STARTS.index(c) + 1] - c)
+                mean_var[c] = stats.tile([P, size, 2], F32, name="mean_var", tag="mean_var_%d" % size)
+                group_of[c] = c
+            else:
+                group_of[c] = group_of[c - 1]
+            first = group_of[c]
             for r in range(TILES):
-                nc.vector.bn_aggr(out=mean_var[c][:, r, :], in_=partial[c][:, r, :])
-            var_eps = stats.tile([P, TILES], F32, name="var_eps")
-            nc.gpsimd.tensor_scalar(
-                out=var_eps[:], in0=mean_var[c][:, :, 1], scalar1=LN_EPS, scalar2=None, op0=ALU.add
-            )
-            rstd[c] = stats.tile([P, TILES], F32, name="rstd")
-            nc.gpsimd.tensor_tensor(out=rstd[c][:], in0=var_eps[:], in1=minus_half[:], op=ALU.pow)
+                nc.vector.bn_aggr(out=mean_var[first][:, TILES * (c - first) + r, :], in_=partial[c][:, r, :])
+            if c + 1 in GROUP_STARTS:
+                size = TILES * (c + 1 - first)
+                var_eps = stats.tile([P, size], F32, name="var_eps", tag="var_eps_%d" % size)
+                nc.gpsimd.tensor_scalar(
+                    out=var_eps[:], in0=mean_var[first][:, :, 1], scalar1=LN_EPS, scalar2=None, op0=ALU.add
+                )
+                rstd[first] = stats.tile([P, size], F32, name="rstd", tag="rstd_%d" % size)
+                nc.gpsimd.tensor_tensor(
+                    out=rstd[first][:], in0=var_eps[:], in1=minus_half[:, 0:size], op=ALU.pow
+                )
 
         def centre_and_scale(c, r):
             if r == 0:
                 zc[c] = work.tile([P, TILES, H], F32, name="zc")
+            first = group_of[c]
+            i = TILES * (c - first) + r
             nc.vector.tensor_scalar(
                 out=zc[c][:, r, :].rearrange("p (j m) -> p j m", j=GROUPS),
                 in0=z_sb[c][:, r * H : (r + 1) * H].rearrange("p (m j) -> p j m", j=GROUPS),
-                scalar1=mean_var[c][:, r, 0:1],
-                scalar2=rstd[c][:, r : r + 1],
+                scalar1=mean_var[first][:, i, 0:1],
+                scalar2=rstd[first][:, i : i + 1],
                 op0=ALU.subtract,
                 op1=ALU.mult,
             )
@@ -312,12 +326,12 @@ def tile_gatedlinearattention_pb_t_kernel(tc, z, hidden_states, Wg, Wo, gamma, b
                 transpose_zc(t + 2, 1)
             if live(t + 3):
                 transpose_hs(t + 3)
-            if live(t + 4):
-                token_sums(t + 4, 0)
-                token_sums(t + 4, 1)
-                token_statistics(t + 4)
+            if live(t + 5):
+                token_sums(t + 5, 0)
+                token_sums(t + 5, 1)
+                token_statistics(t + 5)
             empty_out(t, 0, scopy)
-            empty_out(t, 1, scopy if t < N_CHUNKS - 4 else vcopy)
+            empty_out(t, 1, scopy if t < N_CHUNKS - 5 else vcopy)
             store(t)
             if live(t + 1):
                 gated(t + 1)
@@ -350,6 +364,9 @@ def tile_gatedlinearattention_pb_t_kernel(tc, z, hidden_states, Wg, Wo, gamma, b
             token_sums(2, 0)
             token_sums(2, 1)
             token_statistics(2)
+            token_sums(3, 0)
+            token_sums(3, 1)
+            token_statistics(3)
             gamma_beta(0, 0)
             gamma_beta(0, 1)
             centre_and_scale(1, 0)
@@ -360,13 +377,13 @@ def tile_gatedlinearattention_pb_t_kernel(tc, z, hidden_states, Wg, Wo, gamma, b
             transpose_zc(1, 0)
             transpose_zc(1, 1)
             transpose_hs(2)
-            token_sums(3, 0)
-            token_sums(3, 1)
-            token_statistics(3)
             regroup_wo(scopy, 1)
             gated(0)
             quantise_weight(wo_grouped, wo_codes, wo_scales, 0)
             quantise_weight(wo_grouped, wo_codes, wo_scales, 1)
+            token_sums(4, 0)
+            token_sums(4, 1)
+            token_statistics(4)
 
         for t in range(N_CHUNKS):
             step(t)

from contextlib import ExitStack

import concourse.mybir as mybir
from concourse.masks import make_identity

F32 = mybir.dt.float32
BF16 = mybir.dt.bfloat16
U32 = mybir.dt.uint32
U8 = mybir.dt.uint8
FP8X4 = mybir.dt.float8_e4m3fn_x4
ALU = mybir.AluOpType
ACT = mybir.ActivationFunctionType

P = 128
PACK = 4
H = 512
TOKENS = 16 * 256
HALF = H // 2
TILES = 2
CHUNK = TILES * P
N_CHUNKS = TOKENS // CHUNK
GROUPS = H // P
HALVES = 2
RUN = 4
LN_EPS = 1e-5
GROUP_STARTS = [0, 1] + list(range(2, N_CHUNKS + 1, 2))
STORE_BUFS = 6

FLOPS = 2 * 2 * TOKENS * H * H


def tile_gatedlinearattention_pb_t_kernel(tc, z, hidden_states, Wg, Wo, gamma, beta, out):
    nc = tc.nc

    z_chunks = z.flatten_outer_dims().rearrange("(c p r) f -> c p (r f)", p=P, r=TILES)
    hs_chunks = hidden_states.flatten_outer_dims().rearrange("(c p r) f -> c p (r f)", p=P, r=TILES)
    out_chunks = out.flatten_outer_dims().rearrange("(c p r) f -> c p (r f)", p=P, r=TILES)

    with ExitStack() as stack:
        const = stack.enter_context(tc.tile_pool(name="const", bufs=1))
        inputs = stack.enter_context(tc.tile_pool(name="inputs", bufs=N_CHUNKS))
        work = stack.enter_context(tc.tile_pool(name="work", bufs=3))
        stats = stack.enter_context(tc.tile_pool(name="stats", bufs=6))
        stores = stack.enter_context(tc.tile_pool(name="stores", bufs=STORE_BUFS))
        psum = stack.enter_context(tc.psum_pool(name="psum", bufs=2))

        ident = const.tile([P, P], F32, name="ident")
        make_identity(nc, ident[:])
        minus_half = const.tile([P, 2 * TILES], F32, name="minus_half")
        nc.gpsimd.memset(minus_half[:], -0.5)
        gamma_raw = const.tile([P, GROUPS], BF16, name="gamma_raw")
        beta_raw = const.tile([P, GROUPS], BF16, name="beta_raw")
        gamma_col = const.tile([P, GROUPS], F32, name="gamma_col")
        beta_col = const.tile([P, GROUPS], F32, name="beta_col")

        z_sb = {}
        hs_sb = {}

        def load_z(c):
            z_sb[c] = inputs.tile([P, TILES * H], BF16, name="z_sb")
            nc.sync.dma_start(out=z_sb[c][:], in_=z_chunks[c])

        def load_hs(c):
            hs_sb[c] = inputs.tile([P, TILES * H], BF16, name="hs_sb")
            nc.sync.dma_start(out=hs_sb[c][:], in_=hs_chunks[c])

        wg_raw = const.tile([P, PACK, H], BF16, name="wg_raw")
        wo_raw = const.tile([P, PACK, H], BF16, name="wo_raw")
        load_z(0)
        nc.scalar.dma_start(out=gamma_raw[:], in_=gamma.rearrange("(p j) -> p j", j=GROUPS))
        nc.scalar.dma_start(out=beta_raw[:], in_=beta.rearrange("(p j) -> p j", j=GROUPS))
        load_hs(0)
        nc.sync.dma_start(out=wg_raw[:], in_=Wg.rearrange("(p j) n -> p j n", j=PACK))
        load_z(1)
        load_hs(1)
        nc.sync.dma_start(out=wo_raw[:], in_=Wo.rearrange("(p j) n -> p j n", j=PACK))
        for c in range(2, N_CHUNKS):
            load_z(c)
            load_hs(c)

        table_warmer = const.tile([P, 1], F32, name="table_warmer")
        nc.scalar.activation(out=table_warmer[:], in_=minus_half[:, 0:1], func=ACT.Silu)
        nc.gpsimd.tensor_copy(out=gamma_col[:], in_=gamma_raw[:])
        nc.gpsimd.tensor_copy(out=beta_col[:], in_=beta_raw[:])

        wg_grouped = const.tile([P, H, PACK], BF16, name="wg_grouped", align_bytes=64)
        wg_codes = const.tile([P, H], U32, name="wg_codes", align_bytes=64)
        wg_scales = const.tile([P, H], U8, name="wg_scales", align_bytes=64)
        wo_grouped = const.tile([P, H, PACK], BF16, name="wo_grouped", align_bytes=64)
        wo_codes = const.tile([P, H], U32, name="wo_codes", align_bytes=64)
        wo_scales = const.tile([P, H], U8, name="wo_scales", align_bytes=64)

        def regroup_wg(copy, half):
            copy(
                out=wg_grouped[:, half * HALF : (half + 1) * HALF, :].rearrange("p (j m) t -> p j m t", j=2),
                in_=wg_raw[:].rearrange("p t (m j) -> p j m t", j=GROUPS)[:, 2 * half : 2 * half + 2],
            )

        def regroup_wo(copy, half):
            cols = slice(half * HALF, (half + 1) * HALF)
            copy(
                out=wo_grouped[:, cols, :].rearrange("p (a i) t -> p a t i", i=RUN),
                in_=wo_raw[:, :, cols].rearrange("p t (a i) -> p a t i", i=RUN),
            )

        def quantise_weight(grouped, codes, scales, half):
            cols = slice(half * HALF, (half + 1) * HALF)
            nc.vector.quantize_mx(
                out=codes[:, cols].bitcast(FP8X4),
                scales=scales[:, cols],
                in_=grouped[:, cols, :].rearrange("p n t -> p (n t)"),
            )

        partial = {}
        mean_var = {}
        rstd = {}
        group_of = {}
        zc = {}
        zcT_ps = {}
        hsT_ps = {}
        hs_grouped = {}
        hs_mx = {}
        g_ps = {}
        gate = {}
        zn = {}
        h_grouped = {}
        h_mx = {}
        out_ps = {}
        out_sb = {}

        def token_sums(c, r):
            if r == 0:
                partial[c] = stats.tile([P, TILES, 6], F32, name="partial")
            nc.vector.bn_stats(out=partial[c][:, r, :], in_=z_sb[c][:, r * H : (r + 1) * H])

        def token_statistics(c):
            if c in GROUP_STARTS:
                size = TILES * (GROUP_STARTS[GROUP_STARTS.index(c) + 1] - c)
                mean_var[c] = stats.tile([P, size, 2], F32, name="mean_var", tag="mean_var_%d" % size)
                group_of[c] = c
            else:
                group_of[c] = group_of[c - 1]
            first = group_of[c]
            for r in range(TILES):
                nc.vector.bn_aggr(out=mean_var[first][:, TILES * (c - first) + r, :], in_=partial[c][:, r, :])
            if c + 1 in GROUP_STARTS:
                size = TILES * (c + 1 - first)
                var_eps = stats.tile([P, size], F32, name="var_eps", tag="var_eps_%d" % size)
                nc.gpsimd.tensor_scalar(
                    out=var_eps[:], in0=mean_var[first][:, :, 1], scalar1=LN_EPS, scalar2=None, op0=ALU.add
                )
                rstd[first] = stats.tile([P, size], F32, name="rstd", tag="rstd_%d" % size)
                nc.gpsimd.tensor_tensor(
                    out=rstd[first][:], in0=var_eps[:], in1=minus_half[:, 0:size], op=ALU.pow
                )

        def centre_and_scale(c, r):
            if r == 0:
                zc[c] = work.tile([P, TILES, H], F32, name="zc")
            first = group_of[c]
            i = TILES * (c - first) + r
            nc.vector.tensor_scalar(
                out=zc[c][:, r, :].rearrange("p (j m) -> p j m", j=GROUPS),
                in0=z_sb[c][:, r * H : (r + 1) * H].rearrange("p (m j) -> p j m", j=GROUPS),
                scalar1=mean_var[first][:, i, 0:1],
                scalar2=rstd[first][:, i : i + 1],
                op0=ALU.subtract,
                op1=ALU.mult,
            )

        def transpose_zc(c, pair):
            zcT_ps[c, pair] = psum.tile([P, 2, CHUNK], F32, name="zcT_ps")
            for i in range(2):
                j = 2 * pair + i
                for r in range(TILES):
                    nc.tensor.transpose(
                        zcT_ps[c, pair][:, i, r * P : (r + 1) * P],
                        zc[c][:, r, j * P : (j + 1) * P],
                        ident[:],
                    )

        def transpose_hs(c):
            words = hs_sb[c][:].bitcast(F32)
            hsT_ps[c] = psum.tile([P, HALVES, CHUNK], F32, name="hsT_ps")
            for r in range(TILES):
                for u in range(HALVES):
                    nc.tensor.transpose(
                        hsT_ps[c][:, u, r * P : (r + 1) * P],
                        words[:, r * H // HALVES + u : (r + 1) * H // HALVES : HALVES],
                        ident[:],
                    )

        def regroup_hs(c, copy):
            hs_grouped[c] = work.tile([P, CHUNK * PACK], BF16, name="hs_grouped", align_bytes=64)
            copy(
                out=hs_grouped[c][:].bitcast(F32).rearrange("p (w u) -> p w u", u=HALVES),
                in_=hsT_ps[c][:].rearrange("p u w -> p w u"),
            )

        def quantise(grouped, name):
            codes = work.tile([P, CHUNK], U32, name=name + "_codes", align_bytes=64)
            scales = work.tile([P, CHUNK], U8, name=name + "_scales", align_bytes=64)
            nc.vector.quantize_mx(out=codes[:].bitcast(FP8X4), scales=scales[:], in_=grouped[:])
            return codes, scales

        def quantise_h(c):
            codes = work.tile([P, CHUNK], U32, name="h_codes", align_bytes=64)
            scales = work.tile([P, CHUNK], U8, name="h_scales", align_bytes=64)
            for first, tokens in pieces(c):
                cols = slice(first, first + tokens)
                nc.vector.quantize_mx(
                    out=codes[:, cols].bitcast(FP8X4),
                    scales=scales[:, cols],
                    in_=h_grouped[c][:, first * PACK : (first + tokens) * PACK],
                )
            h_mx[c] = codes, scales

        def first_product(c, pair):
            hs_codes, hs_scales = hs_mx[c]
            g_ps[c, pair] = psum.tile([P, 2, CHUNK], F32, name="g_ps")
            for i in range(2):
                j = 2 * pair + i
                nc.tensor.matmul_mx(
                    out=g_ps[c, pair][:, i, :],
                    lhsT=wg_codes[:, j * P : (j + 1) * P].bitcast(FP8X4),
                    lhsT_scale=wg_scales[:, j * P : (j + 1) * P],
                    rhs=hs_codes[:].bitcast(FP8X4),
                    rhs_scale=hs_scales[:],
                    start=True,
                    stop=True,
                )

        def silu_gate(c, pair):
            if pair == 0:
                gate[c] = work.tile([P, CHUNK // RUN, GROUPS, RUN], F32, name="gate")
            nc.scalar.activation(
                out=gate[c][:, :, 2 * pair : 2 * pair + 2, :].rearrange("p a j i -> p j a i"),
                in_=g_ps[c, pair][:].rearrange("p j (a i) -> p j a i", i=RUN),
                func=ACT.Silu,
            )

        def gamma_beta(c, pair):
            if pair == 0:
                zn[c] = work.tile([P, CHUNK // RUN, GROUPS, RUN], F32, name="zn")
            for i in range(2):
                j = 2 * pair + i
                nc.scalar.activation(
                    out=zn[c][:, :, j, :],
                    in_=zcT_ps[c, pair][:, i, :].rearrange("p (a i) -> p a i", i=RUN),
                    func=ACT.Identity,
                    scale=gamma_col[:, j : j + 1],
                    bias=beta_col[:, j : j + 1],
                )

        def pieces(c):
            return [(0, CHUNK)] if c < N_CHUNKS - 1 else [(r * P, P) for r in range(TILES)]

        def gated(c):
            h_grouped[c] = work.tile([P, CHUNK * PACK], BF16, name="h_grouped", align_bytes=64)
            for first, tokens in pieces(c):
                runs = slice(first // RUN, (first + tokens) // RUN)
                nc.vector.tensor_tensor(
                    out=h_grouped[c][:, first * PACK : (first + tokens) * PACK].rearrange(
                        "p (a i j) -> p a j i", i=RUN, j=PACK
                    ),
                    in0=zn[c][:, runs],
                    in1=gate[c][:, runs],
                    op=ALU.mult,
                )

        def second_product(c, r):
            h_codes, h_scales = h_mx[c]
            out_ps[c, r] = psum.tile([P, H], F32, name="out_ps")
            nc.tensor.matmul_mx(
                out=out_ps[c, r][:],
                lhsT=h_codes[:, r * P : (r + 1) * P].bitcast(FP8X4),
                lhsT_scale=h_scales[:, r * P : (r + 1) * P],
                rhs=wo_codes[:].bitcast(FP8X4),
                rhs_scale=wo_scales[:],
                start=True,
                stop=True,
            )

        def empty_out(c, r, copy):
            if r == 0:
                out_sb[c] = stores.tile([P, TILES * H], F32, name="out_sb")
            copy(out=out_sb[c][:, r * H : (r + 1) * H], in_=out_ps[c, r][:])

        def store(c):
            if c < N_CHUNKS - 1:
                nc.sync.dma_start(out=out_chunks[c], in_=out_sb[c][:])
            else:
                nc.scalar.dma_start(out=out_chunks[c][:, 0:H], in_=out_sb[c][:, 0:H])
                nc.sync.dma_start(out=out_chunks[c][:, H : 2 * H], in_=out_sb[c][:, H : 2 * H])

        vcopy = nc.vector.tensor_copy
        scopy = nc.scalar.copy

        def live(c):
            return 0 <= c < N_CHUNKS

        def hs_copy(c):
            return scopy if c < 4 or c % 2 else vcopy

        def step(t):
            if live(t + 2):
                regroup_hs(t + 2, hs_copy(t + 2))
                centre_and_scale(t + 2, 0)
            quantise_h(t)
            if live(t + 2):
                centre_and_scale(t + 2, 1)
                hs_mx[t + 2] = quantise(hs_grouped[t + 2], "hs")
            if live(t + 1):
                silu_gate(t + 1, 0)
                silu_gate(t + 1, 1)
            second_product(t, 0)
            second_product(t, 1)
            if live(t + 2):
                first_product(t + 2, 0)
                first_product(t + 2, 1)
            if live(t + 1):
                gamma_beta(t + 1, 0)
                gamma_beta(t + 1, 1)
            if live(t + 2):
                transpose_zc(t + 2, 0)
                transpose_zc(t + 2, 1)
            if live(t + 3):
                transpose_hs(t + 3)
            if live(t + 5):
                token_sums(t + 5, 0)
                token_sums(t + 5, 1)
                token_statistics(t + 5)
            empty_out(t, 0, scopy)
            empty_out(t, 1, scopy if t < N_CHUNKS - 5 else vcopy)
            store(t)
            if live(t + 1):
                gated(t + 1)

        with tc.manual_schedule():
            token_sums(0, 0)
            token_sums(0, 1)
            token_statistics(0)
            transpose_hs(0)
            regroup_wg(vcopy, 0)
            regroup_wg(scopy, 1)
            quantise_weight(wg_grouped, wg_codes, wg_scales, 0)
            quantise_weight(wg_grouped, wg_codes, wg_scales, 1)
            regroup_hs(0, hs_copy(0))
            hs_mx[0] = quantise(hs_grouped[0], "hs")
            transpose_hs(1)
            token_sums(1, 0)
            token_sums(1, 1)
            token_statistics(1)
            centre_and_scale(0, 0)
            centre_and_scale(0, 1)
            first_product(0, 0)
            first_product(0, 1)
            regroup_hs(1, hs_copy(1))
            transpose_zc(0, 0)
            transpose_zc(0, 1)
            silu_gate(0, 0)
            silu_gate(0, 1)
            hs_mx[1] = quantise(hs_grouped[1], "hs")
            token_sums(2, 0)
            token_sums(2, 1)
            token_statistics(2)
            token_sums(3, 0)
            token_sums(3, 1)
            token_statistics(3)
            gamma_beta(0, 0)
            gamma_beta(0, 1)
            centre_and_scale(1, 0)
            centre_and_scale(1, 1)
            regroup_wo(scopy, 0)
            first_product(1, 0)
            first_product(1, 1)
            transpose_zc(1, 0)
            transpose_zc(1, 1)
            transpose_hs(2)
            regroup_wo(scopy, 1)
            gated(0)
            quantise_weight(wo_grouped, wo_codes, wo_scales, 0)
            quantise_weight(wo_grouped, wo_codes, wo_scales, 1)
            token_sums(4, 0)
            token_sums(4, 1)
            token_statistics(4)

        for t in range(N_CHUNKS):
            step(t)
